import numpy as np
import ml_dtypes


def mxq(x, axis, fmt="e4m3"):
    dtype, down = {"e4m3": (ml_dtypes.float8_e4m3fn, 7), "e5m2": (ml_dtypes.float8_e5m2, 14)}[fmt]
    v = np.moveaxis(np.asarray(x, np.float32).astype(ml_dtypes.bfloat16).astype(np.float64), axis, -1)
    blocks = v.reshape(v.shape[:-1] + (-1, 32))
    amax = np.abs(blocks).max(-1, keepdims=True)
    byte = np.maximum(np.where(amax > 0, np.frexp(amax)[1] - 1 + 127, 0) - down, 1)
    scale = np.exp2(byte - 127.0)
    codes = (blocks / scale).astype(np.float32).astype(dtype).astype(np.float64)
    return np.moveaxis((codes * scale).reshape(v.shape), -1, axis)


WIDE = False


def mx_kscale(k):
    if not WIDE:
        return np.ones(k)
    levels = np.array([10, -10, 5, -5, 0])
    if k % 512:
        return np.exp2(np.random.permutation(np.resize(levels, k // 32))).repeat(32)
    a = np.empty((k // 512, 16))
    for p in range(k // 512):
        a[p, :8] = np.random.permutation(np.resize(levels, 8))
        for g in range(8):
            far = levels[np.abs(levels - a[p, g]) >= 10]
            a[p, g + 8] = far[np.random.randint(len(far))]
    return np.exp2(a.ravel()).repeat(32)


BF16 = ml_dtypes.bfloat16


def bf(x):
    return np.asarray(x, np.float32).astype(BF16)


def f64(x):
    return np.asarray(x).astype(np.float64)


B, C, NH, GW, GH, GZ = 2, 1024, 2, 16, 8, 8
N = GW * GH * GZ
D = C // NH
XS = 2.0


def draw0():
    s, t = mx_kscale(C), mx_kscale(D)
    g = np.random.standard_normal((B, NH, D, D)) * np.sqrt(1.0 + C / N)
    e = np.exp(g - g.max(-1, keepdims=True))
    attn = e / e.sum(-1, keepdims=True)
    return {"x": bf(XS * np.random.standard_normal((B, C, GW, GH, GZ)) * s[None, :, None, None, None]),
            "w_v": bf(np.random.standard_normal((C, C)) / np.sqrt(C) / s[:, None] * np.tile(t, NH)[None, :]),
            "attn": bf(attn / t)}


def core(x, w_v, attn):
    xt = f64(x).reshape(B, C, N).transpose(0, 2, 1)
    v = mxq(xt, 2, "e4m3") @ mxq(f64(w_v), 0, "e4m3")
    v = v.reshape(B, N, NH, D).transpose(0, 2, 3, 1)
    out = mxq(f64(attn), 3, "e4m3") @ mxq(v, 2, "e4m3")
    out = out.transpose(0, 3, 1, 2).reshape(B, N, C)
    return out.reshape(B, GW, GH, GZ, C).transpose(0, 4, 1, 2, 3)


def e4m3fn_bytes(y):
    return np.clip(np.asarray(y, np.float64), -448.0, 448.0).astype(np.float32).astype(ml_dtypes.float8_e4m3fn).view(np.uint8)


def e4m3fn_values(b):
    return np.asarray(b, np.uint8).view(ml_dtypes.float8_e4m3fn).astype(np.float64)


def setup_inputs():
    d = draw0()
    x0 = np.asarray(d['x']).astype(np.float64)
    s = (np.max(np.abs(x0), axis=(0, 2, 3, 4), keepdims=True) / 448.0).astype(np.float32)
    out = {}
    for k, v in d.items():
        if k == 'x':
            out['x_bytes'] = e4m3fn_bytes(x0 / s.astype(np.float64))
            out['x_scale'] = s
        else:
            out[k] = v
    return out


def reference(x_bytes, x_scale, w_v, attn):
    return core(e4m3fn_values(x_bytes) * x_scale.astype(np.float64), w_v, attn)

@@ -1,0 +1,269 @@
+from contextlib import ExitStack
+
+import concourse.mybir as mybir
+from concourse.masks import make_identity
+
+F32 = mybir.dt.float32
+BF16 = mybir.dt.bfloat16
+U32 = mybir.dt.uint32
+U8 = mybir.dt.uint8
+E4M3FN = mybir.dt.float8_e4m3fn
+FP8X4 = mybir.dt.float8_e4m3fn_x4
+MULT = mybir.AluOpType.mult
+COPY = mybir.ActivationFunctionType.Copy
+
+B, C, NH, N = 2, 1024, 2, 1024
+D = C // NH
+P = 128
+PACK = 4
+KP = P * PACK
+G = C // KP
+FLOPS = 2 * B * N * C * C + 2 * B * NH * D * D * N
+
+UNIT = 256
+Q = 128
+LAG = 4
+
+
+def tile_channelattention_pb_kernel(tc, x_bytes, x_scale, w_v, attn, out):
+    nc = tc.nc
+    with ExitStack() as ctx:
+        keep = ctx.enter_context(tc.tile_pool(name="keep", bufs=1))
+        work = ctx.enter_context(tc.tile_pool(name="work", bufs=2))
+        psum = ctx.enter_context(tc.psum_pool(name="psum", bufs=4))
+
+        x_in = x_bytes.rearrange("b c w h z -> b c (w h z)")
+        out_v = out.rearrange("b c w h z -> b c (w h z)")
+        s_in = x_scale.rearrange("a c w h z -> (a c w h z)").rearrange("(g p t) -> p g t", p=P, t=PACK)
+
+        ident = keep.tile([P, P], F32, name="ident")
+        xs = keep.tile([P, G, 8], F32, name="xs")
+        x_codes = [keep.tile([P, G, N], U32, name="x_codes%d" % b, align_bytes=64) for b in range(B)]
+        x_sc = [keep.tile([P, G, N], U8, name="scx%d" % b, align_bytes=64) for b in range(B)]
+        w_codes = [keep.tile([P, G, D], U32, name="w_codes%d" % h, align_bytes=64) for h in range(NH)]
+        w_sc = [keep.tile([P, G, D], U8, name="scw%d" % h, align_bytes=64) for h in range(NH)]
+        a_codes = [[keep.tile([P, D], U32, name="a_codes%d%d" % (b, h), align_bytes=64) for h in range(NH)] for b in range(B)]
+        a_sc = [[keep.tile([P, D], U8, name="sca%d%d" % (b, h), align_bytes=64) for h in range(NH)] for b in range(B)]
+        w_raw = {}
+        a_raw = {}
+        x_raw = {}
+
+        def load_x(b, n0, width):
+            for g in range(G):
+                xb = keep.tile([P, PACK, width], U8, name="xb_%d_%d_%d" % (b, n0, g), align_bytes=64)
+                x_raw[b, n0, g] = xb
+                nc.sync.dma_start(out=xb[:], in_=x_in[b].rearrange("(g p t) n -> g p t n", p=P, t=PACK)[g][:, :, n0:n0 + width])
+
+        def load_w(h, g):
+            wr = keep.tile([P, PACK, D], BF16, name="w_raw%d%d" % (h, g), align_bytes=64)
+            w_raw[h, g] = wr
+            nc.sync.dma_start(out=wr[:], in_=w_v.rearrange("(g p t) o -> g p t o", p=P, t=PACK)[g][:, :, h * D:(h + 1) * D])
+
+        def load_a(b, h):
+            ar = keep.tile([P, 4, D], BF16, name="a_raw%d%d" % (b, h), align_bytes=64)
+            a_raw[b, h] = ar
+            nc.sync.dma_start(out=ar[:], in_=attn[b][h].rearrange("(i p) j -> p i j", p=P))
+
+        nc.scalar.dma_start(out=xs[:, :, 0:PACK], in_=s_in)
+        load_x(0, 0, 256)
+        load_w(0, 0)
+        load_w(0, 1)
+        load_x(0, 256, 256)
+        load_a(0, 0)
+        load_w(1, 0)
+        load_w(1, 1)
+        load_a(0, 1)
+        load_x(0, 512, 512)
+        load_x(1, 0, 512)
+        load_a(1, 0)
+        load_a(1, 1)
+        load_x(1, 512, 512)
+        make_identity(nc, ident[:])
+
+        x_wide = {}
+        x_grp = {}
+
+        def widen(b, n0, width, g, eng):
+            xw = work.tile([P, PACK, width], BF16, name="xw", bufs=4, align_bytes=64)
+            x_wide[b, n0, g] = xw
+            view = x_raw[b, n0, g][:].bitcast(E4M3FN)
+            for t in range(PACK):
+                if eng == "V":
+                    nc.vector.tensor_scalar(out=xw[:, t, :], in0=view[:, t, :], scalar1=xs[:, g, t:t + 1], scalar2=None, op0=MULT)
+                else:
+                    nc.scalar.activation(out=xw[:, t, :], in_=view[:, t, :], func=COPY, scale=xs[:, g, t:t + 1])
+
+        def x_inter(b, n0, width, g, eng):
+            xg = work.tile([P, width, PACK], BF16, name="xg", bufs=4, align_bytes=64)
+            x_grp[b, n0, g] = xg
+            dst = xg[:].rearrange("p (c i) t -> p c t i", i=4)
+            src = x_wide[b, n0, g][:].rearrange("p t (c i) -> p c t i", i=4)
+            if eng == "V":
+                nc.vector.tensor_copy(out=dst, in_=src)
+            else:
+                nc.scalar.copy(out=dst, in_=src)
+
+        def x_quant(b, n0, width, g):
+            cols = slice(n0, n0 + width)
+            nc.vector.quantize_mx(out=x_codes[b][:, g, cols].bitcast(FP8X4), scales=x_sc[b][:, g, cols], in_=x_grp[b, n0, g][:].rearrange("p n t -> p (n t)"))
+
+        w_grp = {}
+
+        def w_inter(h, g, m0, m1, eng):
+            if (h, g) not in w_grp:
+                wg_tile = work.tile([P, D, PACK], BF16, name="wg", bufs=4, align_bytes=64)
+                w_grp[h, g] = wg_tile
+            dst = w_grp[h, g][:].rearrange("p (t m) j -> p t m j", t=PACK)
+            src = w_raw[h, g][:].rearrange("p j (m t) -> p t m j", t=PACK)
+            if eng == "V":
+                nc.vector.tensor_copy(out=dst[:, :, m0:m1, :], in_=src[:, :, m0:m1, :])
+            else:
+                nc.scalar.copy(out=dst[:, :, m0:m1, :], in_=src[:, :, m0:m1, :])
+
+        def w_quant(h, g):
+            nc.vector.quantize_mx(out=w_codes[h][:, g, :].bitcast(FP8X4), scales=w_sc[h][:, g, :], in_=w_grp[h, g][:].rearrange("p o j -> p (o j)"))
+
+        a_grp = {}
+
+        def a_trans(b, h, half, eng):
+            bank = psum.tile([P, 2, 2, P], F32, name="obank")
+            words = a_raw[b, h][:].rearrange("p i j -> p (i j)").bitcast(F32)
+            for i in range(2):
+                base = (2 * half + i) * (D // 2)
+                for u in range(2):
+                    nc.tensor.transpose(bank[:, i, u, :], words[:, base + u:base + D // 2:2], ident[:])
+            if half == 0:
+                ag_tile = work.tile([P, D, PACK], BF16, name="ag", bufs=4, align_bytes=64)
+                a_grp[b, h] = ag_tile
+            dst = a_grp[b, h][:].rearrange("p i k -> p (i k)").bitcast(F32).rearrange("p (i r u) -> p i r u", r=P, u=2)
+            src = bank[:].rearrange("p i u r -> p i r u")
+            if eng == "V":
+                nc.vector.tensor_copy(out=dst[:, 2 * half:2 * half + 2], in_=src)
+            else:
+                nc.scalar.copy(out=dst[:, 2 * half:2 * half + 2], in_=src)
+
+        def a_quant(b, h):
+            nc.vector.quantize_mx(out=a_codes[b][h][:].bitcast(FP8X4), scales=a_sc[b][h][:], in_=a_grp[b, h][:].rearrange("p i k -> p (i k)"))
+
+        v_grp = {}
+        v_codes = {}
+        v_sc = {}
+        o_tile = {}
+
+        def unit_of(u):
+            return u // 8, (u // 2) % 4, u % 2
+
+        def stage1(s, eng):
+            u, q = s // 2, s % 2
+            b, k, h = unit_of(u)
+            n0 = k * UNIT + q * Q
+            bank = psum.tile([P, PACK, Q], F32, name="vbank")
+            for t in range(PACK):
+                for g in range(G):
+                    wcol = slice(t * P, (t + 1) * P)
+                    nc.tensor.matmul_mx(out=bank[:, t, :], lhsT=w_codes[h][:, g, wcol].bitcast(FP8X4), lhsT_scale=w_sc[h][:, g, wcol],
+                                        rhs=x_codes[b][:, g, n0:n0 + Q].bitcast(FP8X4), rhs_scale=x_sc[b][:, g, n0:n0 + Q],
+                                        start=(g == 0), stop=(g == G - 1))
+            if q == 0:
+                vg_tile = work.tile([P, UNIT, PACK], BF16, name="vg", bufs=4, align_bytes=64)
+                v_grp[u] = vg_tile
+            dst = v_grp[u][:, q * Q:(q + 1) * Q, :]
+            src = bank[:].rearrange("p t n -> p n t")
+            if eng == "V":
+                nc.vector.tensor_copy(out=dst, in_=src)
+            else:
+                nc.scalar.copy(out=dst, in_=src)
+
+        def v_quant(u):
+            vc = work.tile([P, UNIT], U32, name="vc", bufs=4, align_bytes=64)
+            vs = work.tile([P, UNIT], U8, name="scv", bufs=4, align_bytes=64)
+            v_codes[u] = vc
+            v_sc[u] = vs
+            nc.vector.quantize_mx(out=vc[:].bitcast(FP8X4), scales=vs[:], in_=v_grp[u][:].rearrange("p n t -> p (n t)"))
+
+        def stage2(o, eng):
+            u, half = o // 2, o % 2
+            b, k, h = unit_of(u)
+            bank = psum.tile([P, 2, UNIT], F32, name="obank")
+            for i in range(2):
+                icol = slice((2 * half + i) * P, (2 * half + i + 1) * P)
+                nc.tensor.matmul_mx(out=bank[:, i, :], lhsT=a_codes[b][h][:, icol].bitcast(FP8X4), lhsT_scale=a_sc[b][h][:, icol],
+                                    rhs=v_codes[u][:].bitcast(FP8X4), rhs_scale=v_sc[u][:], start=True, stop=True)
+            if k % 2 == 0:
+                ot_tile = work.tile([P, 2, 2 * UNIT], F32, name="ot", bufs=8)
+                o_tile[b, h, half] = ot_tile
+            ot = o_tile[b, h, half]
+            part = slice((k % 2) * UNIT, (k % 2 + 1) * UNIT)
+            if eng == "V":
+                nc.vector.tensor_copy(out=ot[:, :, part], in_=bank[:])
+            else:
+                nc.scalar.copy(out=ot[:, :, part], in_=bank[:])
+            r0 = h * D + half * 2 * P
+            rows = out_v[b][r0:r0 + 2 * P, :].rearrange("(i p) n -> p i n", p=P)
+            if u >= 12:
+                nc.sync.dma_start(out=rows[:, :, k * UNIT:(k + 1) * UNIT], in_=ot[:, :, part])
+            elif k % 2 == 1:
+                nc.sync.dma_start(out=rows[:, :, (k - 1) * UNIT:(k + 1) * UNIT], in_=ot[:])
+
+        def x_steps(b, n0, width, eng="VVVV"):
+            return [lambda: widen(b, n0, width, 0, eng[0]), lambda: widen(b, n0, width, 1, eng[1]),
+                    lambda: x_inter(b, n0, width, 0, eng[2]), lambda: x_inter(b, n0, width, 1, eng[3]),
+                    lambda: x_quant(b, n0, width, 0), lambda: x_quant(b, n0, width, 1)]
+
+        def a_steps(b, h, eng):
+            return [lambda: a_trans(b, h, 0, eng), lambda: a_trans(b, h, 1, eng), lambda: a_quant(b, h)]
+
+        bg = {s: [] for s in range(64)}
+
+        def spread(steps, s0, ns):
+            for k in range(len(steps)):
+                bg[s0 + (k * ns) // len(steps)].append(steps[k])
+
+        with tc.manual_schedule():
+            for g in range(G):
+                widen(0, 0, 256, g, "VS"[g])
+            x_inter(0, 0, 256, 0, "V")
+            w_inter(0, 0, 0, 64, "V")
+            x_inter(0, 0, 256, 1, "V")
+            w_inter(0, 0, 64, 128, "S")
+            x_quant(0, 0, 256, 0)
+            x_quant(0, 0, 256, 1)
+            w_inter(0, 1, 0, 64, "S")
+            w_inter(0, 1, 64, 128, "V")
+            w_quant(0, 0)
+            w_quant(0, 1)
+            widen(0, 256, 256, 0, "S")
+            widen(0, 256, 256, 1, "V")
+            x_inter(0, 256, 256, 0, "S")
+            a_trans(0, 0, 0, "S")
+            w_inter(1, 0, 0, 128, "V")
+            stage1(0, "S")
+            stage1(1, "S")
+            a_trans(0, 0, 1, "S")
+            w_inter(1, 1, 0, 128, "V")
+            w_quant(1, 0)
+            v_quant(0)
+            a_quant(0, 0)
+            w_quant(1, 1)
+            a_trans(0, 1, 0, "S")
+            a_trans(0, 1, 1, "S")
+            x_quant(0, 256, 256, 0)
+            x_inter(0, 256, 256, 1, "S")
+            stage2(0, "S")
+            stage2(1, "S")
+            bg[2] = [lambda: a_quant(0, 1), lambda: widen(0, 512, 512, 0, "V"), lambda: x_quant(0, 256, 256, 1)]
+            spread(x_steps(0, 512, 512)[1:], 3, 5)
+            spread(x_steps(1, 0, 512), 8, 8)
+            spread(a_steps(1, 0, "S"), 6, 6)
+            spread(a_steps(1, 1, "S"), 11, 6)
+            spread(x_steps(1, 512, 512), 16, 7)
+            for s in range(2, 32 + LAG):
+                if s < 32:
+                    stage1(s, "V" if s in (20, 22, 24) else "S")
+                for f in bg[s]:
+                    f()
+                if s % 2 == 1 and s > 2 and s // 2 - 1 < 16 and s // 2 - 1 > 0:
+                    v_quant(s // 2 - 1)
+                o = s - LAG
+                if o >= 2:
+                    stage2(o, "V" if (o >= 19 and o % 2 == 1) else "S")

@@ -37,6 +37,7 @@ def tile_channelattention_pb_kernel(tc, x_bytes, x_scale, w_v, attn, out):
         s_in = x_scale.rearrange("a c w h z -> (a c w h z)").rearrange("(g p t) -> p g t", p=P, t=PACK)
 
         ident = keep.tile([P, P], F32, name="ident")
+        warm = keep.tile([P, 8], F32, name="warm")
         xs = keep.tile([P, G, 8], F32, name="xs")
         x_codes = [keep.tile([P, G, N], U32, name="x_codes%d" % b, align_bytes=64) for b in range(B)]
         x_sc = [keep.tile([P, G, N], U8, name="scx%d" % b, align_bytes=64) for b in range(B)]
@@ -48,10 +49,11 @@ def tile_channelattention_pb_kernel(tc, x_bytes, x_scale, w_v, attn, out):
         a_raw = {}
         x_raw = {}
 
-        def load_x(b, n0, width):
-            for g in range(G):
+        def load_x(b, n0, width, gs=(0, 1)):
+            for g in gs:
                 xb = keep.tile([P, PACK, width], U8, name="xb_%d_%d_%d" % (b, n0, g), align_bytes=64)
-                x_raw[b, n0, g] = xb
+                for n1 in range(n0, n0 + width, 256):
+                    x_raw[b, n1, g] = (n0, xb)
                 nc.sync.dma_start(out=xb[:], in_=x_in[b].rearrange("(g p t) n -> g p t n", p=P, t=PACK)[g][:, :, n0:n0 + width])
 
         def load_w(h, g):
@@ -62,23 +64,24 @@ def tile_channelattention_pb_kernel(tc, x_bytes, x_scale, w_v, attn, out):
         def load_a(b, h):
             ar = keep.tile([P, 4, D], BF16, name="a_raw%d%d" % (b, h), align_bytes=64)
             a_raw[b, h] = ar
-            nc.sync.dma_start(out=ar[:], in_=attn[b][h].rearrange("(i p) j -> p i j", p=P))
+            nc.sync.dma_start(out=ar[:], in_=attn[b][h].rearrange("(p i) j -> p i j", i=4))
 
         nc.scalar.dma_start(out=xs[:, :, 0:PACK], in_=s_in)
-        load_x(0, 0, 256)
+        load_x(0, 0, 512, (0,))
         load_w(0, 0)
+        load_x(0, 0, 512, (1,))
         load_w(0, 1)
-        load_x(0, 256, 256)
-        load_a(0, 0)
         load_w(1, 0)
         load_w(1, 1)
-        load_a(0, 1)
+        load_a(0, 0)
         load_x(0, 512, 512)
-        load_x(1, 0, 512)
+        load_a(0, 1)
+        load_x(1, 0, 1024)
         load_a(1, 0)
         load_a(1, 1)
-        load_x(1, 512, 512)
         make_identity(nc, ident[:])
+        nc.vector.memset(warm[:], 0.0)
+        nc.scalar.activation(out=warm[:], in_=warm[:], func=COPY)
 
         x_wide = {}
         x_grp = {}
@@ -86,7 +89,8 @@ def tile_channelattention_pb_kernel(tc, x_bytes, x_scale, w_v, attn, out):
         def widen(b, n0, width, g, eng):
             xw = work.tile([P, PACK, width], BF16, name="xw", bufs=4, align_bytes=64)
             x_wide[b, n0, g] = xw
-            view = x_raw[b, n0, g][:].bitcast(E4M3FN)
+            base, raw = x_raw[b, n0, g]
+            view = raw[:].bitcast(E4M3FN)[:, :, n0 - base:n0 - base + width]
             for t in range(PACK):
                 if eng == "V":
                     nc.vector.tensor_scalar(out=xw[:, t, :], in0=view[:, t, :], scalar1=xs[:, g, t:t + 1], scalar2=None, op0=MULT)
@@ -113,12 +117,12 @@ def tile_channelattention_pb_kernel(tc, x_bytes, x_scale, w_v, attn, out):
             if (h, g) not in w_grp:
                 wg_tile = work.tile([P, D, PACK], BF16, name="wg", bufs=4, align_bytes=64)
                 w_grp[h, g] = wg_tile
-            dst = w_grp[h, g][:].rearrange("p (t m) j -> p t m j", t=PACK)
-            src = w_raw[h, g][:].rearrange("p j (m t) -> p t m j", t=PACK)
+            dst = w_grp[h, g][:].rearrange("p (t m) j -> p m j t", t=PACK)
+            src = w_raw[h, g][:].rearrange("p j (m t) -> p m j t", t=PACK)
             if eng == "V":
-                nc.vector.tensor_copy(out=dst[:, :, m0:m1, :], in_=src[:, :, m0:m1, :])
+                nc.vector.tensor_copy(out=dst[:, m0:m1], in_=src[:, m0:m1])
             else:
-                nc.scalar.copy(out=dst[:, :, m0:m1, :], in_=src[:, :, m0:m1, :])
+                nc.scalar.copy(out=dst[:, m0:m1], in_=src[:, m0:m1])
 
         def w_quant(h, g):
             nc.vector.quantize_mx(out=w_codes[h][:, g, :].bitcast(FP8X4), scales=w_sc[h][:, g, :], in_=w_grp[h, g][:].rearrange("p o j -> p (o j)"))
@@ -198,8 +202,7 @@ def tile_channelattention_pb_kernel(tc, x_bytes, x_scale, w_v, attn, out):
                 nc.vector.tensor_copy(out=ot[:, :, part], in_=bank[:])
             else:
                 nc.scalar.copy(out=ot[:, :, part], in_=bank[:])
-            r0 = h * D + half * 2 * P
-            rows = out_v[b][r0:r0 + 2 * P, :].rearrange("(i p) n -> p i n", p=P)
+            rows = out_v[b][h * D:(h + 1) * D, :].rearrange("(p i) n -> p i n", i=4)[:, 2 * half:2 * half + 2, :]
             if u >= 12:
                 nc.sync.dma_start(out=rows[:, :, k * UNIT:(k + 1) * UNIT], in_=ot[:, :, part])
             elif k % 2 == 1:
@@ -219,7 +222,7 @@ def tile_channelattention_pb_kernel(tc, x_bytes, x_scale, w_v, attn, out):
             for k in range(len(steps)):
                 bg[s0 + (k * ns) // len(steps)].append(steps[k])
 
-        with tc.manual_schedule():
+        if True:
             for g in range(G):
                 widen(0, 0, 256, g, "VS"[g])
             x_inter(0, 0, 256, 0, "V")

@@ -49,12 +49,14 @@ def tile_channelattention_pb_kernel(tc, x_bytes, x_scale, w_v, attn, out):
         a_raw = {}
         x_raw = {}
 
-        def load_x(b, n0, width, gs=(0, 1)):
+        def load_x(b, n0, width, gs=(0, 1), parts=1):
             for g in gs:
                 xb = keep.tile([P, PACK, width], U8, name="xb_%d_%d_%d" % (b, n0, g), align_bytes=64)
                 for n1 in range(n0, n0 + width, 256):
                     x_raw[b, n1, g] = (n0, xb)
-                nc.sync.dma_start(out=xb[:], in_=x_in[b].rearrange("(g p t) n -> g p t n", p=P, t=PACK)[g][:, :, n0:n0 + width])
+                for i in range(parts):
+                    ts = slice(i * PACK // parts, (i + 1) * PACK // parts)
+                    nc.sync.dma_start(out=xb[:, ts, :], in_=x_in[b].rearrange("(g p t) n -> g p t n", p=P, t=PACK)[g][:, ts, n0:n0 + width])
 
         def load_w(h, g):
             wr = keep.tile([P, PACK, D], BF16, name="w_raw%d%d" % (h, g), align_bytes=64)
@@ -67,18 +69,18 @@ def tile_channelattention_pb_kernel(tc, x_bytes, x_scale, w_v, attn, out):
             nc.sync.dma_start(out=ar[:], in_=attn[b][h].rearrange("(p i) j -> p i j", i=4))
 
         nc.scalar.dma_start(out=xs[:, :, 0:PACK], in_=s_in)
-        load_x(0, 0, 512, (0,))
+        load_x(0, 0, 512, (0,), 2)
         load_w(0, 0)
         load_x(0, 0, 512, (1,))
         load_w(0, 1)
+        load_a(0, 0)
         load_w(1, 0)
         load_w(1, 1)
-        load_a(0, 0)
         load_x(0, 512, 512)
         load_a(0, 1)
-        load_x(1, 0, 1024)
         load_a(1, 0)
         load_a(1, 1)
+        load_x(1, 0, 1024)
         make_identity(nc, ident[:])
         nc.vector.memset(warm[:], 0.0)
         nc.scalar.activation(out=warm[:], in_=warm[:], func=COPY)
@@ -87,7 +89,7 @@ def tile_channelattention_pb_kernel(tc, x_bytes, x_scale, w_v, attn, out):
         x_grp = {}
 
         def widen(b, n0, width, g, eng):
-            xw = work.tile([P, PACK, width], BF16, name="xw", bufs=4, align_bytes=64)
+            xw = work.tile([P, PACK, width], BF16, name="xw", bufs=6, align_bytes=64)
             x_wide[b, n0, g] = xw
             base, raw = x_raw[b, n0, g]
             view = raw[:].bitcast(E4M3FN)[:, :, n0 - base:n0 - base + width]
@@ -98,7 +100,7 @@ def tile_channelattention_pb_kernel(tc, x_bytes, x_scale, w_v, attn, out):
                     nc.scalar.activation(out=xw[:, t, :], in_=view[:, t, :], func=COPY, scale=xs[:, g, t:t + 1])
 
         def x_inter(b, n0, width, g, eng):
-            xg = work.tile([P, width, PACK], BF16, name="xg", bufs=4, align_bytes=64)
+            xg = work.tile([P, width, PACK], BF16, name="xg", bufs=6, align_bytes=64)
             x_grp[b, n0, g] = xg
             dst = xg[:].rearrange("p (c i) t -> p c t i", i=4)
             src = x_wide[b, n0, g][:].rearrange("p t (c i) -> p c t i", i=4)
@@ -129,14 +131,20 @@ def tile_channelattention_pb_kernel(tc, x_bytes, x_scale, w_v, attn, out):
 
         a_grp = {}
 
-        def a_trans(b, h, half, eng):
+        a_bank = {}
+
+        def a_trans(b, h, half):
             bank = psum.tile([P, 2, 2, P], F32, name="obank")
+            a_bank[b, h, half] = bank
             words = a_raw[b, h][:].rearrange("p i j -> p (i j)").bitcast(F32)
             for i in range(2):
                 base = (2 * half + i) * (D // 2)
                 for u in range(2):
                     nc.tensor.transpose(bank[:, i, u, :], words[:, base + u:base + D // 2:2], ident[:])
-            if half == 0:
+
+        def a_copy(b, h, half, eng):
+            bank = a_bank[b, h, half]
+            if (b, h) not in a_grp:
                 ag_tile = work.tile([P, D, PACK], BF16, name="ag", bufs=4, align_bytes=64)
                 a_grp[b, h] = ag_tile
             dst = a_grp[b, h][:].rearrange("p i k -> p (i k)").bitcast(F32).rearrange("p (i r u) -> p i r u", r=P, u=2)
@@ -157,19 +165,28 @@ def tile_channelattention_pb_kernel(tc, x_bytes, x_scale, w_v, attn, out):
         def unit_of(u):
             return u // 8, (u // 2) % 4, u % 2
 
-        def stage1(s, eng):
+        v_bank = {}
+        o_bank = {}
+        o_done = {}
+
+        def stage1(s):
             u, q = s // 2, s % 2
             b, k, h = unit_of(u)
             n0 = k * UNIT + q * Q
             bank = psum.tile([P, PACK, Q], F32, name="vbank")
+            v_bank[s] = bank
             for t in range(PACK):
                 for g in range(G):
                     wcol = slice(t * P, (t + 1) * P)
                     nc.tensor.matmul_mx(out=bank[:, t, :], lhsT=w_codes[h][:, g, wcol].bitcast(FP8X4), lhsT_scale=w_sc[h][:, g, wcol],
                                         rhs=x_codes[b][:, g, n0:n0 + Q].bitcast(FP8X4), rhs_scale=x_sc[b][:, g, n0:n0 + Q],
                                         start=(g == 0), stop=(g == G - 1))
-            if q == 0:
-                vg_tile = work.tile([P, UNIT, PACK], BF16, name="vg", bufs=4, align_bytes=64)
+
+        def v_copy(s, eng):
+            u, q = s // 2, s % 2
+            bank = v_bank[s]
+            if u not in v_grp:
+                vg_tile = work.tile([P, UNIT, PACK], BF16, name="vg", bufs=8, align_bytes=64)
                 v_grp[u] = vg_tile
             dst = v_grp[u][:, q * Q:(q + 1) * Q, :]
             src = bank[:].rearrange("p t n -> p n t")
@@ -179,34 +196,43 @@ def tile_channelattention_pb_kernel(tc, x_bytes, x_scale, w_v, attn, out):
                 nc.scalar.copy(out=dst, in_=src)
 
         def v_quant(u):
-            vc = work.tile([P, UNIT], U32, name="vc", bufs=4, align_bytes=64)
-            vs = work.tile([P, UNIT], U8, name="scv", bufs=4, align_bytes=64)
+            vc = work.tile([P, UNIT], U32, name="vc", bufs=6, align_bytes=64)
+            vs = work.tile([P, UNIT], U8, name="scv", bufs=6, align_bytes=64)
             v_codes[u] = vc
             v_sc[u] = vs
             nc.vector.quantize_mx(out=vc[:].bitcast(FP8X4), scales=vs[:], in_=v_grp[u][:].rearrange("p n t -> p (n t)"))
 
-        def stage2(o, eng):
+        def stage2(o):
             u, half = o // 2, o % 2
             b, k, h = unit_of(u)
             bank = psum.tile([P, 2, UNIT], F32, name="obank")
+            o_bank[o] = bank
             for i in range(2):
                 icol = slice((2 * half + i) * P, (2 * half + i + 1) * P)
                 nc.tensor.matmul_mx(out=bank[:, i, :], lhsT=a_codes[b][h][:, icol].bitcast(FP8X4), lhsT_scale=a_sc[b][h][:, icol],
                                     rhs=v_codes[u][:].bitcast(FP8X4), rhs_scale=v_sc[u][:], start=True, stop=True)
-            if k % 2 == 0:
+
+        def o_copy(o, eng):
+            u, half = o // 2, o % 2
+            b, k, h = unit_of(u)
+            bank = o_bank[o]
+            key = (b, h, half, k // 2)
+            if key not in o_tile:
                 ot_tile = work.tile([P, 2, 2 * UNIT], F32, name="ot", bufs=8)
-                o_tile[b, h, half] = ot_tile
-            ot = o_tile[b, h, half]
+                o_tile[key] = ot_tile
+                o_done[key] = 0
+            ot = o_tile[key]
+            o_done[key] = o_done[key] + 1
             part = slice((k % 2) * UNIT, (k % 2 + 1) * UNIT)
             if eng == "V":
                 nc.vector.tensor_copy(out=ot[:, :, part], in_=bank[:])
             else:
                 nc.scalar.copy(out=ot[:, :, part], in_=bank[:])
             rows = out_v[b][h * D:(h + 1) * D, :].rearrange("(p i) n -> p i n", i=4)[:, 2 * half:2 * half + 2, :]
-            if u >= 12:
+            if key in SPLIT:
                 nc.sync.dma_start(out=rows[:, :, k * UNIT:(k + 1) * UNIT], in_=ot[:, :, part])
-            elif k % 2 == 1:
-                nc.sync.dma_start(out=rows[:, :, (k - 1) * UNIT:(k + 1) * UNIT], in_=ot[:])
+            elif o_done[key] == 2:
+                nc.sync.dma_start(out=rows[:, :, (k // 2) * 2 * UNIT:(k // 2 + 1) * 2 * UNIT], in_=ot[:])
 
         def x_steps(b, n0, width, eng="VVVV"):
             return [lambda: widen(b, n0, width, 0, eng[0]), lambda: widen(b, n0, width, 1, eng[1]),
@@ -216,57 +242,217 @@ def tile_channelattention_pb_kernel(tc, x_bytes, x_scale, w_v, attn, out):
         def a_steps(b, h, eng):
             return [lambda: a_trans(b, h, 0, eng), lambda: a_trans(b, h, 1, eng), lambda: a_quant(b, h)]
 
+        SPLIT = [(1, 0, 0, 1), (1, 0, 1, 1), (1, 1, 0, 1), (1, 1, 1, 1)]
         bg = {s: [] for s in range(64)}
 
         def spread(steps, s0, ns):
             for k in range(len(steps)):
                 bg[s0 + (k * ns) // len(steps)].append(steps[k])
 
-        if True:
-            for g in range(G):
-                widen(0, 0, 256, g, "VS"[g])
+        with tc.manual_schedule():
+            widen(0, 0, 256, 0, "V")
             x_inter(0, 0, 256, 0, "V")
             w_inter(0, 0, 0, 64, "V")
-            x_inter(0, 0, 256, 1, "V")
-            w_inter(0, 0, 64, 128, "S")
-            x_quant(0, 0, 256, 0)
-            x_quant(0, 0, 256, 1)
-            w_inter(0, 1, 0, 64, "S")
-            w_inter(0, 1, 64, 128, "V")
-            w_quant(0, 0)
-            w_quant(0, 1)
             widen(0, 256, 256, 0, "S")
-            widen(0, 256, 256, 1, "V")
             x_inter(0, 256, 256, 0, "S")
-            a_trans(0, 0, 0, "S")
-            w_inter(1, 0, 0, 128, "V")
-            stage1(0, "S")
-            stage1(1, "S")
-            a_trans(0, 0, 1, "S")
-            w_inter(1, 1, 0, 128, "V")
-            w_quant(1, 0)
-            v_quant(0)
-            a_quant(0, 0)
-            w_quant(1, 1)
-            a_trans(0, 1, 0, "S")
-            a_trans(0, 1, 1, "S")
+            widen(0, 256, 256, 1, "S")
+            widen(0, 0, 256, 1, "S")
+            w_inter(0, 0, 64, 128, "V")
+            w_inter(0, 1, 0, 64, "S")
+            a_trans(0,0,0)
+            x_quant(0, 0, 256, 0)
+            a_trans(0,0,1)
+            w_quant(0,0)
+            w_inter(0, 1, 64, 128, "V")
+            w_inter(1, 0, 0, 64, "S")
+            w_inter(1, 1, 64, 128, "S")
+            a_copy(0,0,0, "S")
+            x_inter(0, 256, 256, 1, "V")
+            x_inter(0, 0, 256, 1, "V")
             x_quant(0, 256, 256, 0)
-            x_inter(0, 256, 256, 1, "S")
-            stage2(0, "S")
-            stage2(1, "S")
-            bg[2] = [lambda: a_quant(0, 1), lambda: widen(0, 512, 512, 0, "V"), lambda: x_quant(0, 256, 256, 1)]
-            spread(x_steps(0, 512, 512)[1:], 3, 5)
-            spread(x_steps(1, 0, 512), 8, 8)
-            spread(a_steps(1, 0, "S"), 6, 6)
-            spread(a_steps(1, 1, "S"), 11, 6)
-            spread(x_steps(1, 512, 512), 16, 7)
-            for s in range(2, 32 + LAG):
-                if s < 32:
-                    stage1(s, "V" if s in (20, 22, 24) else "S")
-                for f in bg[s]:
-                    f()
-                if s % 2 == 1 and s > 2 and s // 2 - 1 < 16 and s // 2 - 1 > 0:
-                    v_quant(s // 2 - 1)
-                o = s - LAG
-                if o >= 2:
-                    stage2(o, "V" if (o >= 19 and o % 2 == 1) else "S")
+            a_copy(0,0,1, "S")
+            x_quant(0, 0, 256, 1)
+            w_quant(0,1)
+            w_inter(1, 0, 64, 128, "V")
+            x_quant(0, 256, 256, 1)
+            w_inter(1, 1, 0, 64, "V")
+            w_quant(1,0)
+            w_quant(1,1)
+            widen(0, 512, 512, 0, "V")
+            widen(0, 512, 512, 1, "V")
+            stage1(0)
+            x_inter(0, 512, 512, 0, "V")
+            v_copy(0, "S")
+            stage1(1)
+            x_inter(0, 512, 512, 1, "V")
+            v_copy(1, "S")
+            stage1(2)
+            a_quant(0,0)
+            x_quant(0, 512, 512, 0)
+            v_quant(0)
+            v_copy(2, "S")
+            stage1(3)
+            a_trans(0,1,0)
+            a_trans(0,1,1)
+            a_trans(1,0,0)
+            x_quant(0, 512, 512, 1)
+            a_trans(1,0,1)
+            v_copy(3, "S")
+            a_copy(0,1,0, "S")
+            stage1(4)
+            a_copy(0,1,1, "S")
+            a_copy(1,0,0, "S")
+            a_copy(1,0,1, "S")
+            v_quant(1)
+            v_copy(4, "S")
+            stage1(5)
+            a_trans(1,1,0)
+            a_trans(1,1,1)
+            stage2(0)
+            a_quant(0,1)
+            v_copy(5, "S")
+            stage1(6)
+            a_quant(1,0)
+            a_copy(1,1,0, "S")
+            a_copy(1,1,1, "S")
+            stage2(1)
+            v_quant(2)
+            o_copy(0, "S")
+            v_copy(6, "S")
+            widen(1, 0, 512, 0, "V")
+            stage1(7)
+            stage2(2)
+            o_copy(1, "S")
+            v_copy(7, "S")
+            stage1(8)
+            a_quant(1,1)
+            widen(1, 0, 512, 1, "V")
+            stage2(3)
+            o_copy(2, "S")
+            v_quant(3)
+            v_copy(8, "S")
+            stage1(9)
+            stage2(4)
+            o_copy(3, "S")
+            x_inter(1, 0, 512, 0, "V")
+            v_copy(9, "S")
+            stage1(10)
+            stage2(5)
+            o_copy(4, "S")
+            v_quant(4)
+            x_inter(1, 0, 512, 1, "V")
+            v_copy(10, "S")
+            stage1(11)
+            stage2(6)
+            o_copy(5, "S")
+            v_copy(11, "S")
+            stage1(12)
+            stage2(7)
+            o_copy(6, "S")
+            x_quant(1, 0, 512, 0)
+            v_quant(5)
+            stage2(8)
+            v_copy(12, "S")
+            stage1(13)
+            o_copy(7, "V")
+            x_quant(1, 0, 512, 1)
+            stage2(9)
+            v_copy(13, "S")
+            stage1(14)
+            o_copy(8, "S")
+            stage2(10)
+            v_quant(6)
+            v_copy(14, "S")
+            o_copy(9, "S")
+            stage1(15)
+            stage2(11)
+            o_copy(10, "S")
+            v_copy(15, "S")
+            stage1(16)
+            widen(1, 512, 512, 0, "V")
+            stage2(12)
+            o_copy(11, "V")
+            v_quant(7)
+            v_copy(16, "S")
+            stage1(17)
+            stage2(13)
+            o_copy(12, "S")
+            widen(1, 512, 512, 1, "V")
+            v_copy(17, "S")
+            stage1(18)
+            stage2(14)
+            o_copy(13, "S")
+            v_quant(8)
+            v_copy(18, "S")
+            stage1(19)
+            stage2(15)
+            x_inter(1, 512, 512, 0, "V")
+            o_copy(14, "S")
+            v_copy(19, "S")
+            stage1(20)
+            stage2(16)
+            o_copy(15, "V")
+            v_quant(9)
+            x_inter(1, 512, 512, 1, "V")
+            v_copy(20, "S")
+            stage1(21)
+            stage2(17)
+            o_copy(16, "S")
+            v_copy(21, "S")
+            stage2(18)
+            stage1(22)
+            o_copy(17, "S")
+            x_quant(1, 512, 512, 0)
+            v_quant(10)
+            stage2(19)
+            v_copy(22, "S")
+            stage1(23)
+            o_copy(18, "S")
+            stage2(20)
+            x_quant(1, 512, 512, 1)
+            v_copy(23, "V")
+            stage1(24)
+            o_copy(19, "V")
+            stage2(21)
+            v_quant(11)
+            o_copy(20, "S")
+            v_copy(24, "S")
+            stage1(25)
+            stage2(22)
+            o_copy(21, "S")
+            v_copy(25, "V")
+            stage1(26)
+            stage2(23)
+            o_copy(22, "S")
+            v_quant(12)
+            v_copy(26, "S")
+            stage1(27)
+            stage2(24)
+            o_copy(23, "V")
+            v_copy(27, "V")
+            stage1(28)
+            stage2(25)
+            o_copy(24, "S")
+            v_quant(13)
+            v_copy(28, "S")
+            stage1(29)
+            stage2(26)
+            o_copy(25, "S")
+            v_copy(29, "V")
+            stage1(30)
+            stage2(27)
+            o_copy(26, "S")
+            v_quant(14)
+            v_copy(30, "S")
+            stage1(31)
+            stage2(28)
+            o_copy(27, "V")
+            stage2(29)
+            v_copy(31, "V")
+            o_copy(28, "S")
+            v_quant(15)
+            stage2(30)
+            o_copy(29, "S")
+            stage2(31)
+            o_copy(30, "S")
+            o_copy(31, "V")

from contextlib import ExitStack

import concourse.mybir as mybir
from concourse.masks import make_identity

F32 = mybir.dt.float32
BF16 = mybir.dt.bfloat16
U32 = mybir.dt.uint32
U8 = mybir.dt.uint8
E4M3FN = mybir.dt.float8_e4m3fn
FP8X4 = mybir.dt.float8_e4m3fn_x4
MULT = mybir.AluOpType.mult
COPY = mybir.ActivationFunctionType.Copy

B, C, NH, N = 2, 1024, 2, 1024
D = C // NH
P = 128
PACK = 4
KP = P * PACK
G = C // KP
FLOPS = 2 * B * N * C * C + 2 * B * NH * D * D * N

UNIT = 256
Q = 128
LAG = 4


def tile_channelattention_pb_kernel(tc, x_bytes, x_scale, w_v, attn, out):
    nc = tc.nc
    with ExitStack() as ctx:
        keep = ctx.enter_context(tc.tile_pool(name="keep", bufs=1))
        work = ctx.enter_context(tc.tile_pool(name="work", bufs=2))
        psum = ctx.enter_context(tc.psum_pool(name="psum", bufs=4))

        x_in = x_bytes.rearrange("b c w h z -> b c (w h z)")
        out_v = out.rearrange("b c w h z -> b c (w h z)")
        s_in = x_scale.rearrange("a c w h z -> (a c w h z)").rearrange("(g p t) -> p g t", p=P, t=PACK)

        ident = keep.tile([P, P], F32, name="ident")
        warm = keep.tile([P, 8], F32, name="warm")
        xs = keep.tile([P, G, 8], F32, name="xs")
        x_codes = [keep.tile([P, G, N], U32, name="x_codes%d" % b, align_bytes=64) for b in range(B)]
        x_sc = [keep.tile([P, G, N], U8, name="scx%d" % b, align_bytes=64) for b in range(B)]
        w_codes = [keep.tile([P, G, D], U32, name="w_codes%d" % h, align_bytes=64) for h in range(NH)]
        w_sc = [keep.tile([P, G, D], U8, name="scw%d" % h, align_bytes=64) for h in range(NH)]
        a_codes = [[keep.tile([P, D], U32, name="a_codes%d%d" % (b, h), align_bytes=64) for h in range(NH)] for b in range(B)]
        a_sc = [[keep.tile([P, D], U8, name="sca%d%d" % (b, h), align_bytes=64) for h in range(NH)] for b in range(B)]
        w_raw = {}
        a_raw = {}
        x_raw = {}

        def load_x(b, n0, width, gs=(0, 1), parts=1):
            for g in gs:
                xb = keep.tile([P, PACK, width], U8, name="xb_%d_%d_%d" % (b, n0, g), align_bytes=64)
                for n1 in range(n0, n0 + width, 256):
                    x_raw[b, n1, g] = (n0, xb)
                for i in range(parts):
                    ts = slice(i * PACK // parts, (i + 1) * PACK // parts)
                    nc.sync.dma_start(out=xb[:, ts, :], in_=x_in[b].rearrange("(g p t) n -> g p t n", p=P, t=PACK)[g][:, ts, n0:n0 + width])

        def load_w(h, g):
            wr = keep.tile([P, PACK, D], BF16, name="w_raw%d%d" % (h, g), align_bytes=64)
            w_raw[h, g] = wr
            nc.sync.dma_start(out=wr[:], in_=w_v.rearrange("(g p t) o -> g p t o", p=P, t=PACK)[g][:, :, h * D:(h + 1) * D])

        def load_a(b, h):
            ar = keep.tile([P, 4, D], BF16, name="a_raw%d%d" % (b, h), align_bytes=64)
            a_raw[b, h] = ar
            nc.sync.dma_start(out=ar[:], in_=attn[b][h].rearrange("(p i) j -> p i j", i=4))

        nc.scalar.dma_start(out=xs[:, :, 0:PACK], in_=s_in)
        load_x(0, 0, 512, (0,), 2)
        load_w(0, 0)
        load_x(0, 0, 512, (1,))
        load_w(0, 1)
        load_a(0, 0)
        load_w(1, 0)
        load_w(1, 1)
        load_x(0, 512, 512)
        load_a(0, 1)
        load_a(1, 0)
        load_a(1, 1)
        load_x(1, 0, 1024)
        make_identity(nc, ident[:])
        nc.vector.memset(warm[:], 0.0)
        nc.scalar.activation(out=warm[:], in_=warm[:], func=COPY)

        x_wide = {}
        x_grp = {}

        def widen(b, n0, width, g, eng):
            xw = work.tile([P, PACK, width], BF16, name="xw", bufs=6, align_bytes=64)
            x_wide[b, n0, g] = xw
            base, raw = x_raw[b, n0, g]
            view = raw[:].bitcast(E4M3FN)[:, :, n0 - base:n0 - base + width]
            for t in range(PACK):
                if eng == "V":
                    nc.vector.tensor_scalar(out=xw[:, t, :], in0=view[:, t, :], scalar1=xs[:, g, t:t + 1], scalar2=None, op0=MULT)
                else:
                    nc.scalar.activation(out=xw[:, t, :], in_=view[:, t, :], func=COPY, scale=xs[:, g, t:t + 1])

        def x_inter(b, n0, width, g, eng):
            xg = work.tile([P, width, PACK], BF16, name="xg", bufs=6, align_bytes=64)
            x_grp[b, n0, g] = xg
            dst = xg[:].rearrange("p (c i) t -> p c t i", i=4)
            src = x_wide[b, n0, g][:].rearrange("p t (c i) -> p c t i", i=4)
            if eng == "V":
                nc.vector.tensor_copy(out=dst, in_=src)
            else:
                nc.scalar.copy(out=dst, in_=src)

        def x_quant(b, n0, width, g):
            cols = slice(n0, n0 + width)
            nc.vector.quantize_mx(out=x_codes[b][:, g, cols].bitcast(FP8X4), scales=x_sc[b][:, g, cols], in_=x_grp[b, n0, g][:].rearrange("p n t -> p (n t)"))

        w_grp = {}

        def w_inter(h, g, m0, m1, eng):
            if (h, g) not in w_grp:
                wg_tile = work.tile([P, D, PACK], BF16, name="wg", bufs=4, align_bytes=64)
                w_grp[h, g] = wg_tile
            dst = w_grp[h, g][:].rearrange("p (t m) j -> p m j t", t=PACK)
            src = w_raw[h, g][:].rearrange("p j (m t) -> p m j t", t=PACK)
            if eng == "V":
                nc.vector.tensor_copy(out=dst[:, m0:m1], in_=src[:, m0:m1])
            else:
                nc.scalar.copy(out=dst[:, m0:m1], in_=src[:, m0:m1])

        def w_quant(h, g):
            nc.vector.quantize_mx(out=w_codes[h][:, g, :].bitcast(FP8X4), scales=w_sc[h][:, g, :], in_=w_grp[h, g][:].rearrange("p o j -> p (o j)"))

        a_grp = {}

        a_bank = {}

        def a_trans(b, h, half):
            bank = psum.tile([P, 2, 2, P], F32, name="obank")
            a_bank[b, h, half] = bank
            words = a_raw[b, h][:].rearrange("p i j -> p (i j)").bitcast(F32)
            for i in range(2):
                base = (2 * half + i) * (D // 2)
                for u in range(2):
                    nc.tensor.transpose(bank[:, i, u, :], words[:, base + u:base + D // 2:2], ident[:])

        def a_copy(b, h, half, eng):
            bank = a_bank[b, h, half]
            if (b, h) not in a_grp:
                ag_tile = work.tile([P, D, PACK], BF16, name="ag", bufs=4, align_bytes=64)
                a_grp[b, h] = ag_tile
            dst = a_grp[b, h][:].rearrange("p i k -> p (i k)").bitcast(F32).rearrange("p (i r u) -> p i r u", r=P, u=2)
            src = bank[:].rearrange("p i u r -> p i r u")
            if eng == "V":
                nc.vector.tensor_copy(out=dst[:, 2 * half:2 * half + 2], in_=src)
            else:
                nc.scalar.copy(out=dst[:, 2 * half:2 * half + 2], in_=src)

        def a_quant(b, h):
            nc.vector.quantize_mx(out=a_codes[b][h][:].bitcast(FP8X4), scales=a_sc[b][h][:], in_=a_grp[b, h][:].rearrange("p i k -> p (i k)"))

        v_grp = {}
        v_codes = {}
        v_sc = {}
        o_tile = {}

        def unit_of(u):
            return u // 8, (u // 2) % 4, u % 2

        v_bank = {}
        o_bank = {}
        o_done = {}

        def stage1(s):
            u, q = s // 2, s % 2
            b, k, h = unit_of(u)
            n0 = k * UNIT + q * Q
            bank = psum.tile([P, PACK, Q], F32, name="vbank")
            v_bank[s] = bank
            for t in range(PACK):
                for g in range(G):
                    wcol = slice(t * P, (t + 1) * P)
                    nc.tensor.matmul_mx(out=bank[:, t, :], lhsT=w_codes[h][:, g, wcol].bitcast(FP8X4), lhsT_scale=w_sc[h][:, g, wcol],
                                        rhs=x_codes[b][:, g, n0:n0 + Q].bitcast(FP8X4), rhs_scale=x_sc[b][:, g, n0:n0 + Q],
                                        start=(g == 0), stop=(g == G - 1))

        def v_copy(s, eng):
            u, q = s // 2, s % 2
            bank = v_bank[s]
            if u not in v_grp:
                vg_tile = work.tile([P, UNIT, PACK], BF16, name="vg", bufs=8, align_bytes=64)
                v_grp[u] = vg_tile
            dst = v_grp[u][:, q * Q:(q + 1) * Q, :]
            src = bank[:].rearrange("p t n -> p n t")
            if eng == "V":
                nc.vector.tensor_copy(out=dst, in_=src)
            else:
                nc.scalar.copy(out=dst, in_=src)

        def v_quant(u):
            vc = work.tile([P, UNIT], U32, name="vc", bufs=6, align_bytes=64)
            vs = work.tile([P, UNIT], U8, name="scv", bufs=6, align_bytes=64)
            v_codes[u] = vc
            v_sc[u] = vs
            nc.vector.quantize_mx(out=vc[:].bitcast(FP8X4), scales=vs[:], in_=v_grp[u][:].rearrange("p n t -> p (n t)"))

        def stage2(o):
            u, half = o // 2, o % 2
            b, k, h = unit_of(u)
            bank = psum.tile([P, 2, UNIT], F32, name="obank")
            o_bank[o] = bank
            for i in range(2):
                icol = slice((2 * half + i) * P, (2 * half + i + 1) * P)
                nc.tensor.matmul_mx(out=bank[:, i, :], lhsT=a_codes[b][h][:, icol].bitcast(FP8X4), lhsT_scale=a_sc[b][h][:, icol],
                                    rhs=v_codes[u][:].bitcast(FP8X4), rhs_scale=v_sc[u][:], start=True, stop=True)

        def o_copy(o, eng):
            u, half = o // 2, o % 2
            b, k, h = unit_of(u)
            bank = o_bank[o]
            key = (b, h, half, k // 2)
            if key not in o_tile:
                ot_tile = work.tile([P, 2, 2 * UNIT], F32, name="ot", bufs=8)
                o_tile[key] = ot_tile
                o_done[key] = 0
            ot = o_tile[key]
            o_done[key] = o_done[key] + 1
            part = slice((k % 2) * UNIT, (k % 2 + 1) * UNIT)
            if eng == "V":
                nc.vector.tensor_copy(out=ot[:, :, part], in_=bank[:])
            else:
                nc.scalar.copy(out=ot[:, :, part], in_=bank[:])
            rows = out_v[b][h * D:(h + 1) * D, :].rearrange("(p i) n -> p i n", i=4)[:, 2 * half:2 * half + 2, :]
            if key in SPLIT:
                nc.sync.dma_start(out=rows[:, :, k * UNIT:(k + 1) * UNIT], in_=ot[:, :, part])
            elif o_done[key] == 2:
                nc.sync.dma_start(out=rows[:, :, (k // 2) * 2 * UNIT:(k // 2 + 1) * 2 * UNIT], in_=ot[:])

        def x_steps(b, n0, width, eng="VVVV"):
            return [lambda: widen(b, n0, width, 0, eng[0]), lambda: widen(b, n0, width, 1, eng[1]),
                    lambda: x_inter(b, n0, width, 0, eng[2]), lambda: x_inter(b, n0, width, 1, eng[3]),
                    lambda: x_quant(b, n0, width, 0), lambda: x_quant(b, n0, width, 1)]

        def a_steps(b, h, eng):
            return [lambda: a_trans(b, h, 0, eng), lambda: a_trans(b, h, 1, eng), lambda: a_quant(b, h)]

        SPLIT = [(1, 0, 0, 1), (1, 0, 1, 1), (1, 1, 0, 1), (1, 1, 1, 1)]
        bg = {s: [] for s in range(64)}

        def spread(steps, s0, ns):
            for k in range(len(steps)):
                bg[s0 + (k * ns) // len(steps)].append(steps[k])

        with tc.manual_schedule():
            widen(0, 0, 256, 0, "V")
            x_inter(0, 0, 256, 0, "V")
            w_inter(0, 0, 0, 64, "V")
            widen(0, 256, 256, 0, "S")
            x_inter(0, 256, 256, 0, "S")
            widen(0, 256, 256, 1, "S")
            widen(0, 0, 256, 1, "S")
            w_inter(0, 0, 64, 128, "V")
            w_inter(0, 1, 0, 64, "S")
            a_trans(0,0,0)
            x_quant(0, 0, 256, 0)
            a_trans(0,0,1)
            w_quant(0,0)
            w_inter(0, 1, 64, 128, "V")
            w_inter(1, 0, 0, 64, "S")
            w_inter(1, 1, 64, 128, "S")
            a_copy(0,0,0, "S")
            x_inter(0, 256, 256, 1, "V")
            x_inter(0, 0, 256, 1, "V")
            x_quant(0, 256, 256, 0)
            a_copy(0,0,1, "S")
            x_quant(0, 0, 256, 1)
            w_quant(0,1)
            w_inter(1, 0, 64, 128, "V")
            x_quant(0, 256, 256, 1)
            w_inter(1, 1, 0, 64, "V")
            w_quant(1,0)
            w_quant(1,1)
            widen(0, 512, 512, 0, "V")
            widen(0, 512, 512, 1, "V")
            stage1(0)
            x_inter(0, 512, 512, 0, "V")
            v_copy(0, "S")
            stage1(1)
            x_inter(0, 512, 512, 1, "V")
            v_copy(1, "S")
            stage1(2)
            a_quant(0,0)
            x_quant(0, 512, 512, 0)
            v_quant(0)
            v_copy(2, "S")
            stage1(3)
            a_trans(0,1,0)
            a_trans(0,1,1)
            a_trans(1,0,0)
            x_quant(0, 512, 512, 1)
            a_trans(1,0,1)
            v_copy(3, "S")
            a_copy(0,1,0, "S")
            stage1(4)
            a_copy(0,1,1, "S")
            a_copy(1,0,0, "S")
            a_copy(1,0,1, "S")
            v_quant(1)
            v_copy(4, "S")
            stage1(5)
            a_trans(1,1,0)
            a_trans(1,1,1)
            stage2(0)
            a_quant(0,1)
            v_copy(5, "S")
            stage1(6)
            a_quant(1,0)
            a_copy(1,1,0, "S")
            a_copy(1,1,1, "S")
            stage2(1)
            v_quant(2)
            o_copy(0, "S")
            v_copy(6, "S")
            widen(1, 0, 512, 0, "V")
            stage1(7)
            stage2(2)
            o_copy(1, "S")
            v_copy(7, "S")
            stage1(8)
            a_quant(1,1)
            widen(1, 0, 512, 1, "V")
            stage2(3)
            o_copy(2, "S")
            v_quant(3)
            v_copy(8, "S")
            stage1(9)
            stage2(4)
            o_copy(3, "S")
            x_inter(1, 0, 512, 0, "V")
            v_copy(9, "S")
            stage1(10)
            stage2(5)
            o_copy(4, "S")
            v_quant(4)
            x_inter(1, 0, 512, 1, "V")
            v_copy(10, "S")
            stage1(11)
            stage2(6)
            o_copy(5, "S")
            v_copy(11, "S")
            stage1(12)
            stage2(7)
            o_copy(6, "S")
            x_quant(1, 0, 512, 0)
            v_quant(5)
            stage2(8)
            v_copy(12, "S")
            stage1(13)
            o_copy(7, "V")
            x_quant(1, 0, 512, 1)
            stage2(9)
            v_copy(13, "S")
            stage1(14)
            o_copy(8, "S")
            stage2(10)
            v_quant(6)
            v_copy(14, "S")
            o_copy(9, "S")
            stage1(15)
            stage2(11)
            o_copy(10, "S")
            v_copy(15, "S")
            stage1(16)
            widen(1, 512, 512, 0, "V")
            stage2(12)
            o_copy(11, "V")
            v_quant(7)
            v_copy(16, "S")
            stage1(17)
            stage2(13)
            o_copy(12, "S")
            widen(1, 512, 512, 1, "V")
            v_copy(17, "S")
            stage1(18)
            stage2(14)
            o_copy(13, "S")
            v_quant(8)
            v_copy(18, "S")
            stage1(19)
            stage2(15)
            x_inter(1, 512, 512, 0, "V")
            o_copy(14, "S")
            v_copy(19, "S")
            stage1(20)
            stage2(16)
            o_copy(15, "V")
            v_quant(9)
            x_inter(1, 512, 512, 1, "V")
            v_copy(20, "S")
            stage1(21)
            stage2(17)
            o_copy(16, "S")
            v_copy(21, "S")
            stage2(18)
            stage1(22)
            o_copy(17, "S")
            x_quant(1, 512, 512, 0)
            v_quant(10)
            stage2(19)
            v_copy(22, "S")
            stage1(23)
            o_copy(18, "S")
            stage2(20)
            x_quant(1, 512, 512, 1)
            v_copy(23, "V")
            stage1(24)
            o_copy(19, "V")
            stage2(21)
            v_quant(11)
            o_copy(20, "S")
            v_copy(24, "S")
            stage1(25)
            stage2(22)
            o_copy(21, "S")
            v_copy(25, "V")
            stage1(26)
            stage2(23)
            o_copy(22, "S")
            v_quant(12)
            v_copy(26, "S")
            stage1(27)
            stage2(24)
            o_copy(23, "V")
            v_copy(27, "V")
            stage1(28)
            stage2(25)
            o_copy(24, "S")
            v_quant(13)
            v_copy(28, "S")
            stage1(29)
            stage2(26)
            o_copy(25, "S")
            v_copy(29, "V")
            stage1(30)
            stage2(27)
            o_copy(26, "S")
            v_quant(14)
            v_copy(30, "S")
            stage1(31)
            stage2(28)
            o_copy(27, "V")
            stage2(29)
            v_copy(31, "V")
            o_copy(28, "S")
            v_quant(15)
            stage2(30)
            o_copy(29, "S")
            stage2(31)
            o_copy(30, "S")
            o_copy(31, "V")
